import numpy as np
import ml_dtypes


def mxq(x, axis, fmt="e4m3"):
    dtype, down = {"e4m3": (ml_dtypes.float8_e4m3fn, 7), "e5m2": (ml_dtypes.float8_e5m2, 14)}[fmt]
    v = np.moveaxis(np.asarray(x, np.float32).astype(ml_dtypes.bfloat16).astype(np.float64), axis, -1)
    blocks = v.reshape(v.shape[:-1] + (-1, 32))
    amax = np.abs(blocks).max(-1, keepdims=True)
    byte = np.maximum(np.where(amax > 0, np.frexp(amax)[1] - 1 + 127, 0) - down, 1)
    scale = np.exp2(byte - 127.0)
    codes = (blocks / scale).astype(np.float32).astype(dtype).astype(np.float64)
    return np.moveaxis((codes * scale).reshape(v.shape), -1, axis)


WIDE = False


def mx_kscale(k):
    if not WIDE:
        return np.ones(k)
    levels = np.array([10, -10, 5, -5, 0])
    a = np.random.permutation(np.resize(levels, k // 512 * 4)).reshape(k // 512, 4)
    idx = np.arange(k)
    return np.exp2(a[idx // 512, idx % 128 // 32])


BF16 = ml_dtypes.bfloat16


def bf(x):
    return np.asarray(x, np.float32).astype(BF16)


def f64(x):
    return np.asarray(x).astype(np.float64)


B, N, C, O = 2, 512, 512, 256
G = 3 * C


def setup_inputs():
    s, t = mx_kscale(N), mx_kscale(C)
    return {"adjacent": bf(np.random.random((B, N, N)) * np.sqrt(3.0 / N) * s),
            "annotations": bf(np.random.standard_normal((B, N, C)) / s[:, None] * t),
            "gc_bias": bf(np.random.standard_normal((1, 1, C)) * 0.3 * t),
            "gru_W": bf(np.random.standard_normal((C, G)) / np.sqrt(C) / t[:, None]),
            "gru_b_x": bf(np.random.standard_normal(G) * 0.3)}


def reference(adjacent, annotations, gc_bias, gru_W, gru_b_x):
    msg = (mxq(f64(adjacent), 2, "e4m3") @ mxq(f64(annotations), 1, "e4m3")) + f64(gc_bias)
    x = msg.reshape(-1, C)
    return (mxq(x, 1, "e4m3") @ mxq(f64(gru_W), 0, "e4m3")) + f64(gru_b_x)

@@ -1,0 +1,360 @@
+from contextlib import ExitStack
+
+import concourse.masks as masks
+import concourse.mybir as mybir
+
+F32 = mybir.dt.float32
+BF16 = mybir.dt.bfloat16
+U32 = mybir.dt.uint32
+U8 = mybir.dt.uint8
+FP8X4 = mybir.dt.float8_e4m3fn_x4
+ADD = mybir.AluOpType.add
+MULT = mybir.AluOpType.mult
+IDENT = mybir.ActivationFunctionType.Identity
+
+P = 128
+B, N, C, G = 2, 512, 512, 1536
+GT = G // 512
+FLOPS = 2 * B * N * N * C + 2 * B * N * C * G
+
+ORDER = [
+    ("L_adj", 0),
+    ("d_gcb",),
+    ("L_ann", 0),
+    ("d_brow",),
+    ("L_W", 0),
+    ("ident",),
+    ("L_adj", 1),
+    ("L_ann", 1),
+    ("L_W", 1),
+    ("L_W", 2),
+    ("identb",),
+    ("T", 0, 1),
+    ("T", 0, 0),
+    ("EA", 0, 1, "S"),
+    ("RA", 0, 0, "V"),
+    ("BX", 0),
+    ("EA", 0, 0, "S"),
+    ("BX", 1),
+    ("RA", 0, 1, "V"),
+    ("bx", 0, "S"),
+    ("BX", 2),
+    ("QN", 0, 0),
+    ("RW", 0, 256, 256, "S"),
+    ("QN", 0, 1),
+    ("QA", 0, 0),
+    ("RW", 0, 0, 256, "V"),
+    ("T", 1, 0),
+    ("bx", 1, "S"),
+    ("QA", 0, 1),
+    ("S1", 0, 0),
+    ("QW", 0),
+    ("bx", 2, "S"),
+    ("S1", 0, 1),
+    ("T", 1, 1),
+    ("EM", 0, 0),
+    ("RA", 1, 0, "S"),
+    ("EM", 0, 1),
+    ("S1", 0, 2),
+    ("QM", 0, 0),
+    ("RW", 1, 0, 256, "S"),
+    ("S1", 0, 3),
+    ("EM", 0, 2),
+    ("S2", 0, 0, 0),
+    ("QM", 0, 1),
+    ("QM", 0, 2),
+    ("EO", 0, 0, 0, "V"),
+    ("RW", 1, 256, 256, "S"),
+    ("S2", 0, 1, 0),
+    ("S2", 0, 2, 0),
+    ("EM", 0, 3),
+    ("ST", 0, 0, 0),
+    ("QN", 1, 0),
+    ("RA", 1, 1, "S"),
+    ("QW", 1),
+    ("EO", 0, 1, 0, "V"),
+    ("EA", 1, 0, "S"),
+    ("S2", 0, 1, 1),
+    ("QN", 1, 1),
+    ("S2", 0, 0, 1),
+    ("ST", 0, 1, 0),
+    ("EO", 0, 2, 0, "S"),
+    ("S2", 0, 2, 1),
+    ("QM", 0, 3),
+    ("QA", 1, 0),
+    ("EO", 0, 0, 1, "V"),
+    ("EA", 1, 1, "S"),
+    ("S2", 0, 3, 0),
+    ("GA", 0, 2, 0),
+    ("S1", 1, 0),
+    ("EO", 0, 2, 1, "V"),
+    ("EO", 0, 1, 1, "S"),
+    ("ST", 0, 0, 1),
+    ("S1", 1, 1),
+    ("EM", 1, 0),
+    ("RW", 2, 0, 256, "S"),
+    ("ST", 0, 2, 1),
+    ("S2", 0, 3, 1),
+    ("GA", 0, 1, 1),
+    ("ST", 0, 2, 0),
+    ("EO", 0, 3, 0, "V"),
+    ("QA", 1, 1),
+    ("RW", 2, 256, 256, "S"),
+    ("ST", 0, 3, 0),
+    ("EO", 0, 3, 1, "V"),
+    ("ST", 0, 1, 1),
+    ("S1", 1, 2),
+    ("QM", 1, 0),
+    ("ST", 0, 3, 1),
+    ("EM", 1, 1),
+    ("S2", 1, 0, 0),
+    ("EM", 1, 2),
+    ("S2", 1, 0, 1),
+    ("EO", 1, 0, 0, "S"),
+    ("S1", 1, 3),
+    ("QM", 1, 1),
+    ("QM", 1, 2),
+    ("EO", 1, 0, 1, "V"),
+    ("GA", 1, 0, 0),
+    ("S2", 1, 1, 0),
+    ("S2", 1, 2, 1),
+    ("EM", 1, 3),
+    ("ST", 1, 0, 1),
+    ("S2", 1, 2, 0),
+    ("EO", 1, 2, 1, "S"),
+    ("S2", 1, 1, 1),
+    ("EO", 1, 1, 0, "V"),
+    ("ST", 1, 0, 0),
+    ("GA", 1, 2, 1),
+    ("QM", 1, 3),
+    ("ST", 1, 1, 0),
+    ("EO", 1, 2, 0, "V"),
+    ("S2", 1, 3, 0),
+    ("QW", 2),
+    ("S2", 1, 3, 1),
+    ("ST", 1, 2, 0),
+    ("EO", 1, 3, 0, "S"),
+    ("ST", 1, 2, 1),
+    ("EO", 1, 1, 1, "V"),
+    ("S2", 0, 1, 2),
+    ("GA", 1, 3, 0),
+    ("EO", 1, 3, 1, "V"),
+    ("ST", 1, 1, 1),
+    ("S2", 0, 0, 2),
+    ("EO", 0, 1, 2, "S"),
+    ("S2", 0, 3, 2),
+    ("EO", 0, 0, 2, "V"),
+    ("ST", 1, 3, 1),
+    ("S2", 1, 0, 2),
+    ("S2", 0, 2, 2),
+    ("GA", 0, 1, 2),
+    ("ST", 1, 3, 0),
+    ("EO", 0, 3, 2, "V"),
+    ("EO", 1, 0, 2, "S"),
+    ("ST", 0, 0, 2),
+    ("S2", 1, 3, 2),
+    ("EO", 0, 2, 2, "V"),
+    ("EO", 1, 3, 2, "S"),
+    ("S2", 1, 1, 2),
+    ("ST", 0, 3, 2),
+    ("GA", 1, 0, 2),
+    ("S2", 1, 2, 2),
+    ("ST", 0, 1, 2),
+    ("EO", 1, 1, 2, "V"),
+    ("ST", 0, 2, 2),
+    ("EO", 1, 2, 2, "V"),
+    ("ST", 1, 1, 2),
+    ("GA", 1, 3, 2),
+    ("ST", 1, 0, 2),
+    ("ST", 1, 2, 2),
+    ("ST", 1, 3, 2),
+]
+
+
+def tile_gatedgraphconvolution_pa_kernel(tc, adjacent, annotations, gc_bias, gru_W, gru_b_x, out):
+    nc = tc.nc
+    with ExitStack() as ctx:
+        keep = ctx.enter_context(tc.tile_pool(name="keep", bufs=1))
+        ps_tp = ctx.enter_context(tc.psum_pool(name="ps_tp", bufs=2))
+        ps_s1 = ctx.enter_context(tc.psum_pool(name="ps_s1", bufs=2))
+        ps_s2 = ctx.enter_context(tc.psum_pool(name="ps_s2", bufs=4))
+        ctx.enter_context(tc.manual_schedule())
+
+        bv = keep.tile([P, 12], BF16, name="bv")
+        gcb = keep.tile([P, 4], BF16, name="gcb")
+        gcf = keep.tile([P, 4], F32, name="gcf")
+        ident = keep.tile([P, P], F32, name="ident")
+        identb = keep.tile([P, P], BF16, name="identb")
+        bx = keep.tile([P, G], F32, name="bx")
+        adj_raw = [keep.tile([P, 4 * N], BF16, name="adj_raw%d" % b) for b in range(B)]
+        ann_raw = [keep.tile([P, 4 * C], BF16, name="ann_raw%d" % b) for b in range(B)]
+        w_raw = [keep.tile([P, 4 * 512], BF16, name="w_raw%d" % g) for g in range(GT)]
+        msg_pl = [keep.tile([P, 4 * N], BF16, name="msg_pl%d" % b) for b in range(B)]
+        adj_grp = [keep.tile([P, 4 * N], BF16, name="adj_grp%d" % b, align_bytes=64) for b in range(B)]
+        ann_grp = [keep.tile([P, 4 * C], BF16, name="ann_grp%d" % b, align_bytes=64) for b in range(B)]
+        msg_grp = [keep.tile([P, 4 * N], BF16, name="msg_grp%d" % b, align_bytes=64) for b in range(B)]
+        w_grp = [keep.tile([P, 4 * 512], BF16, name="w_grp%d" % g, align_bytes=64) for g in range(GT)]
+        adj_q = [keep.tile([P, N], U32, name="adj_q%d" % b, align_bytes=64) for b in range(B)]
+        ann_q = [keep.tile([P, C], U32, name="ann_q%d" % b, align_bytes=64) for b in range(B)]
+        msg_q = [keep.tile([P, N], U32, name="msg_q%d" % b, align_bytes=64) for b in range(B)]
+        w_q = [keep.tile([P, 512], U32, name="w_q%d" % g, align_bytes=64) for g in range(GT)]
+        adj_s = [keep.tile([P, N], U8, name="adj_s%d" % b, align_bytes=64) for b in range(B)]
+        ann_s = [keep.tile([P, C], U8, name="ann_s%d" % b, align_bytes=64) for b in range(B)]
+        msg_s = [keep.tile([P, N], U8, name="msg_s%d" % b, align_bytes=64) for b in range(B)]
+        w_s = [keep.tile([P, 512], U8, name="w_s%d" % g, align_bytes=64) for g in range(GT)]
+        o_sb = keep.tile([P, B * 4 * G], F32, name="o_sb")
+        out_v = out.rearrange("(b p r) g -> b r p g", b=B, r=4)
+        live = {}
+
+        def copy_on(eng, dst, src):
+            if eng == "V":
+                nc.vector.tensor_copy(out=dst, in_=src)
+            elif eng == "S":
+                nc.scalar.copy(out=dst, in_=src)
+            else:
+                nc.gpsimd.tensor_scalar(out=dst, in0=src, scalar1=1.0, scalar2=0.0, op0=MULT, op1=ADD)
+
+        def quantise(grp, q, s, col0, ncol):
+            nc.vector.quantize_mx(
+                out=q[:, col0 : col0 + ncol].bitcast(FP8X4),
+                scales=s[:, col0 : col0 + ncol],
+                in_=grp[:, 4 * col0 : 4 * (col0 + ncol)],
+            )
+
+        def regroup(eng, grp, raw, col0, ncol):
+            dst = grp[:].rearrange("p (c i t) -> p c t i", i=4, t=4)
+            src = raw[:].rearrange("p (t c i) -> p c t i", t=4, i=4)
+            copy_on(eng, dst[:, col0 // 4 : (col0 + ncol) // 4], src[:, col0 // 4 : (col0 + ncol) // 4])
+
+        def mx(dst, lq, ls, lcols, rq, rs, rcols):
+            nc.tensor.matmul_mx(
+                out=dst,
+                lhsT=lq[:, lcols].bitcast(FP8X4),
+                lhsT_scale=ls[:, lcols],
+                rhs=rq[:, rcols].bitcast(FP8X4),
+                rhs_scale=rs[:, rcols],
+                start=True,
+                stop=True,
+            )
+
+        def obank(b, r, g):
+            o0 = ((b * 4 + r) * GT + g) * 512
+            return o_sb[:, o0 : o0 + 512]
+
+        for op in ORDER:
+            k = op[0]
+            if k == "d_gcb":
+                with nc.allow_non_contiguous_dma(reason="512 bias values, one channel a partition"):
+                    nc.scalar.dma_start(out=gcb[:], in_=gc_bias.rearrange("a b (t p) -> p (a b t)", p=P))
+            elif k == "d_brow":
+                nc.scalar.dma_start(out=bv[:], in_=gru_b_x.rearrange("(p x) -> p x", x=12))
+            elif k == "ident":
+                masks.make_identity(nc, ident[:])
+            elif k == "identb":
+                nc.vector.tensor_copy(out=identb[:], in_=ident[:])
+            elif k == "gcf":
+                nc.vector.tensor_copy(out=gcf[:], in_=gcb[:])
+            elif k == "L_adj":
+                b = op[1]
+                nc.sync.dma_start(out=adj_raw[b][:], in_=adjacent[b].rearrange("(p r) m -> p (r m)", r=4))
+            elif k == "L_ann":
+                b = op[1]
+                nc.sync.dma_start(
+                    out=ann_raw[b][:].rearrange("q (u x) -> q u x", u=2),
+                    in_=annotations[b].rearrange("(u q e) c -> q u (e c)", u=2, e=2),
+                )
+            elif k == "L_W":
+                g = op[1]
+                nc.sync.dma_start(
+                    out=w_raw[g][:].rearrange("p (t x) -> p t x", t=4),
+                    in_=gru_W[:, 512 * g : 512 * g + 512].rearrange("(t p) x -> p t x", p=P),
+                )
+            elif k == "BX":
+                xb = op[1]
+                pb = ps_s2.tile([P, 4, P], F32, name="acc")
+                live[("BX", xb)] = pb
+                for xi in range(4):
+                    x = 4 * xb + xi
+                    nc.tensor.matmul(out=pb[:, xi, :], lhsT=bv[:, x : x + 1].to_broadcast([P, P]), rhs=identb[:], start=True, stop=True)
+            elif k == "bx":
+                xb, eng = op[1], op[2]
+                dst = bx[:].rearrange("m (n x) -> m n x", x=12)[:, :, 4 * xb : 4 * xb + 4]
+                copy_on(eng, dst, live[("BX", xb)][:].rearrange("m x n -> m n x"))
+            elif k == "T":
+                b, h = op[1], op[2]
+                words = adj_raw[b][:].bitcast(F32)
+                xt = ps_tp.tile([P, 2, 2, P], F32, name="xt")
+                live[("T", b, h)] = xt
+                for r2 in range(2):
+                    for u in range(2):
+                        w0 = (2 * h + r2) * 256 + u * 128
+                        nc.tensor.transpose(xt[:, r2, u, :], words[:, w0 : w0 + 128], ident[:])
+            elif k == "EA":
+                b, h, eng = op[1], op[2], op[3]
+                dst = adj_grp[b][:].bitcast(F32).rearrange("q (r p u) -> q r p u", r=4, u=2)
+                copy_on(eng, dst[:, 2 * h : 2 * h + 2], live[("T", b, h)][:].rearrange("q r u p -> q r p u"))
+            elif k == "QA":
+                b, h = op[1], op[2]
+                quantise(adj_grp[b], adj_q[b], adj_s[b], 256 * h, 256)
+            elif k == "RA":
+                b, h, eng = op[1], op[2], op[3]
+                regroup(eng, ann_grp[b], ann_raw[b], 256 * h, 256)
+            elif k == "QN":
+                b, h = op[1], op[2]
+                quantise(ann_grp[b], ann_q[b], ann_s[b], 256 * h, 256)
+            elif k == "RW":
+                g, c0, nco, eng = op[1], op[2], op[3], op[4]
+                regroup(eng, w_grp[g], w_raw[g], c0, nco)
+            elif k == "QW":
+                g = op[1]
+                quantise(w_grp[g], w_q[g], w_s[g], 0, 512)
+            elif k == "S1":
+                b, r = op[1], op[2]
+                bank = ps_s1.tile([P, 4, P], F32, name="bank")
+                live[("S1", b, r)] = bank
+                for t in range(4):
+                    mx(bank[:, t, :], ann_q[b], ann_s[b], slice(P * t, P * t + P), adj_q[b], adj_s[b], slice(P * r, P * r + P))
+            elif k == "EM":
+                b, r = op[1], op[2]
+                nc.vector.tensor_tensor(
+                    out=msg_grp[b][:, 4 * P * r : 4 * P * (r + 1)].rearrange("p (j t) -> p j t", t=4),
+                    in0=live[("S1", b, r)][:].rearrange("p t j -> p j t"),
+                    in1=gcb[:].unsqueeze(1).to_broadcast([P, P, 4]),
+                    op=ADD,
+                )
+            elif k == "QM":
+                b, r = op[1], op[2]
+                quantise(msg_grp[b], msg_q[b], msg_s[b], P * r, P)
+            elif k == "S1t":
+                b, t = op[1], op[2]
+                bank = ps_s1.tile([P, 512], F32, name="bank")
+                live[("S1t", b, t)] = bank
+                mx(bank[:], ann_q[b], ann_s[b], slice(P * t, P * t + P), adj_q[b], adj_s[b], slice(0, 512))
+            elif k == "EMs":
+                b, t = op[1], op[2]
+                nc.scalar.activation(out=msg_pl[b][:, 512 * t : 512 * t + 512], in_=live[("S1t", b, t)][:], func=IDENT, bias=gcf[:, t : t + 1], scale=1.0)
+            elif k == "RM":
+                b, h, eng = op[1], op[2], op[3]
+                regroup(eng, msg_grp[b], msg_pl[b], 256 * h, 256)
+            elif k == "QMh":
+                b, h = op[1], op[2]
+                quantise(msg_grp[b], msg_q[b], msg_s[b], 256 * h, 256)
+            elif k == "S2":
+                b, r, g = op[1], op[2], op[3]
+                acc = ps_s2.tile([P, 512], F32, name="acc")
+                live[("S2", b, r, g)] = acc
+                mx(acc[:], msg_q[b], msg_s[b], slice(P * r, P * r + P), w_q[g], w_s[g], slice(0, 512))
+            elif k == "EO":
+                b, r, g, eng = op[1], op[2], op[3], op[4]
+                if eng == "V":
+                    nc.vector.tensor_tensor(out=obank(b, r, g), in0=live[("S2", b, r, g)][:], in1=bx[:, 512 * g : 512 * g + 512], op=ADD)
+                else:
+                    nc.scalar.copy(out=obank(b, r, g), in_=live[("S2", b, r, g)][:])
+            elif k == "GA":
+                b, r, g = op[1], op[2], op[3]
+                nc.gpsimd.tensor_tensor(out=obank(b, r, g), in0=obank(b, r, g), in1=bx[:, 512 * g : 512 * g + 512], op=ADD)
+            elif k == "ST":
+                b, r, g = op[1], op[2], op[3]
+                nc.sync.dma_start(out=out_v[b, r, :, 512 * g : 512 * g + 512], in_=obank(b, r, g))
+            else:
+                assert False, k

@@ -20,8 +20,8 @@ FLOPS = 2 * B * N * N * C + 2 * B * N * C * G
 ORDER = [
     ("L_adj", 0),
     ("d_gcb",),
-    ("L_ann", 0),
     ("d_brow",),
+    ("L_ann", 0),
     ("L_W", 0),
     ("ident",),
     ("L_adj", 1),
@@ -29,144 +29,137 @@ ORDER = [
     ("L_W", 1),
     ("L_W", 2),
     ("identb",),
-    ("T", 0, 1),
+    ("gcf",),
     ("T", 0, 0),
-    ("EA", 0, 1, "S"),
-    ("RA", 0, 0, "V"),
     ("BX", 0),
     ("EA", 0, 0, "S"),
-    ("BX", 1),
+    ("T", 0, 1),
     ("RA", 0, 1, "V"),
     ("bx", 0, "S"),
+    ("BX", 1),
+    ("RA", 0, 0, "V"),
+    ("EA", 0, 1, "S"),
     ("BX", 2),
-    ("QN", 0, 0),
     ("RW", 0, 256, 256, "S"),
-    ("QN", 0, 1),
     ("QA", 0, 0),
-    ("RW", 0, 0, 256, "V"),
-    ("T", 1, 0),
-    ("bx", 1, "S"),
     ("QA", 0, 1),
-    ("S1", 0, 0),
-    ("QW", 0),
-    ("bx", 2, "S"),
-    ("S1", 0, 1),
+    ("RW", 0, 0, 256, "V"),
     ("T", 1, 1),
+    ("bx", 1, "S"),
+    ("QN", 0, 0),
+    ("QN", 0, 1),
+    ("T", 1, 0),
+    ("bx", 2, "S"),
+    ("QW", 0),
+    ("S1", 0, 0),
+    ("EA", 1, 1, "S"),
+    ("S1", 0, 1),
     ("EM", 0, 0),
-    ("RA", 1, 0, "S"),
+    ("EA", 1, 0, "S"),
     ("EM", 0, 1),
+    ("RA", 1, 0, "S"),
     ("S1", 0, 2),
     ("QM", 0, 0),
-    ("RW", 1, 0, 256, "S"),
     ("S1", 0, 3),
     ("EM", 0, 2),
     ("S2", 0, 0, 0),
+    ("RW", 1, 0, 256, "S"),
     ("QM", 0, 1),
     ("QM", 0, 2),
     ("EO", 0, 0, 0, "V"),
-    ("RW", 1, 256, 256, "S"),
     ("S2", 0, 1, 0),
     ("S2", 0, 2, 0),
-    ("EM", 0, 3),
+    ("QA", 1, 0),
+    ("RW", 1, 256, 256, "S"),
     ("ST", 0, 0, 0),
     ("QN", 1, 0),
+    ("QA", 1, 1),
+    ("EO", 0, 1, 0, "V"),
+    ("S1t", 1, 0),
     ("RA", 1, 1, "S"),
     ("QW", 1),
-    ("EO", 0, 1, 0, "V"),
-    ("EA", 1, 0, "S"),
-    ("S2", 0, 1, 1),
-    ("QN", 1, 1),
-    ("S2", 0, 0, 1),
     ("ST", 0, 1, 0),
-    ("EO", 0, 2, 0, "S"),
-    ("S2", 0, 2, 1),
-    ("QM", 0, 3),
-    ("QA", 1, 0),
-    ("EO", 0, 0, 1, "V"),
-    ("EA", 1, 1, "S"),
-    ("S2", 0, 3, 0),
-    ("GA", 0, 2, 0),
-    ("S1", 1, 0),
-    ("EO", 0, 2, 1, "V"),
-    ("EO", 0, 1, 1, "S"),
-    ("ST", 0, 0, 1),
-    ("S1", 1, 1),
-    ("EM", 1, 0),
-    ("RW", 2, 0, 256, "S"),
-    ("ST", 0, 2, 1),
-    ("S2", 0, 3, 1),
-    ("GA", 0, 1, 1),
+    ("EO", 0, 2, 0, "V"),
+    ("EMs", 1, 0),
+    ("S2", 0, 0, 1),
+    ("QN", 1, 1),
+    ("S2", 0, 1, 1),
     ("ST", 0, 2, 0),
-    ("EO", 0, 3, 0, "V"),
-    ("QA", 1, 1),
+    ("S2", 0, 2, 1),
+    ("EO", 0, 0, 1, "V"),
+    ("RW", 2, 0, 256, "S"),
+    ("EM", 0, 3),
+    ("ST", 0, 0, 1),
+    ("EO", 0, 2, 1, "V"),
     ("RW", 2, 256, 256, "S"),
-    ("ST", 0, 3, 0),
-    ("EO", 0, 3, 1, "V"),
+    ("S1t", 1, 1),
+    ("S1t", 1, 2),
+    ("QM", 0, 3),
+    ("ST", 0, 2, 1),
+    ("EO", 0, 1, 1, "V"),
+    ("S2", 0, 3, 0),
+    ("EMs", 1, 1),
+    ("QW", 2),
+    ("S2", 0, 3, 1),
     ("ST", 0, 1, 1),
-    ("S1", 1, 2),
-    ("QM", 1, 0),
+    ("EMs", 1, 2),
+    ("EO", 0, 3, 0, "V"),
+    ("S1t", 1, 3),
+    ("S2", 0, 0, 2),
+    ("EO", 0, 3, 1, "V"),
+    ("EMs", 1, 3),
+    ("S2", 0, 1, 2),
+    ("ST", 0, 3, 0),
+    ("S2", 0, 2, 2),
+    ("EO", 0, 0, 2, "V"),
     ("ST", 0, 3, 1),
-    ("EM", 1, 1),
-    ("S2", 1, 0, 0),
-    ("EM", 1, 2),
+    ("S2", 0, 3, 2),
+    ("RM", 1, 0, "S"),
+    ("EO", 0, 1, 2, "V"),
+    ("ST", 0, 0, 2),
+    ("EO", 0, 2, 2, "V"),
+    ("ST", 0, 1, 2),
+    ("RM", 1, 1, "S"),
+    ("QMh", 1, 0),
+    ("ST", 0, 2, 2),
+    ("EO", 0, 3, 2, "V"),
     ("S2", 1, 0, 1),
-    ("EO", 1, 0, 0, "S"),
-    ("S1", 1, 3),
-    ("QM", 1, 1),
-    ("QM", 1, 2),
-    ("EO", 1, 0, 1, "V"),
-    ("GA", 1, 0, 0),
+    ("S2", 1, 0, 0),
+    ("QMh", 1, 1),
+    ("ST", 0, 3, 2),
     ("S2", 1, 1, 0),
-    ("S2", 1, 2, 1),
-    ("EM", 1, 3),
+    ("EO", 1, 0, 1, "V"),
+    ("S2", 1, 1, 1),
+    ("EO", 1, 0, 0, "V"),
     ("ST", 1, 0, 1),
     ("S2", 1, 2, 0),
-    ("EO", 1, 2, 1, "S"),
-    ("S2", 1, 1, 1),
     ("EO", 1, 1, 0, "V"),
+    ("S2", 1, 2, 1),
     ("ST", 1, 0, 0),
-    ("GA", 1, 2, 1),
-    ("QM", 1, 3),
-    ("ST", 1, 1, 0),
     ("EO", 1, 2, 0, "V"),
+    ("ST", 1, 1, 0),
     ("S2", 1, 3, 0),
-    ("QW", 2),
-    ("S2", 1, 3, 1),
-    ("ST", 1, 2, 0),
-    ("EO", 1, 3, 0, "S"),
-    ("ST", 1, 2, 1),
     ("EO", 1, 1, 1, "V"),
-    ("S2", 0, 1, 2),
-    ("GA", 1, 3, 0),
-    ("EO", 1, 3, 1, "V"),
+    ("ST", 1, 2, 0),
+    ("EO", 1, 3, 0, "V"),
+    ("S2", 1, 3, 1),
     ("ST", 1, 1, 1),
-    ("S2", 0, 0, 2),
-    ("EO", 0, 1, 2, "S"),
-    ("S2", 0, 3, 2),
-    ("EO", 0, 0, 2, "V"),
-    ("ST", 1, 3, 1),
     ("S2", 1, 0, 2),
-    ("S2", 0, 2, 2),
-    ("GA", 0, 1, 2),
+    ("EO", 1, 2, 1, "V"),
     ("ST", 1, 3, 0),
-    ("EO", 0, 3, 2, "V"),
-    ("EO", 1, 0, 2, "S"),
-    ("ST", 0, 0, 2),
-    ("S2", 1, 3, 2),
-    ("EO", 0, 2, 2, "V"),
-    ("EO", 1, 3, 2, "S"),
+    ("EO", 1, 3, 1, "V"),
+    ("ST", 1, 2, 1),
     ("S2", 1, 1, 2),
-    ("ST", 0, 3, 2),
-    ("GA", 1, 0, 2),
     ("S2", 1, 2, 2),
-    ("ST", 0, 1, 2),
-    ("EO", 1, 1, 2, "V"),
-    ("ST", 0, 2, 2),
+    ("EO", 1, 0, 2, "V"),
+    ("ST", 1, 3, 1),
+    ("S2", 1, 3, 2),
     ("EO", 1, 2, 2, "V"),
-    ("ST", 1, 1, 2),
-    ("GA", 1, 3, 2),
     ("ST", 1, 0, 2),
+    ("EO", 1, 1, 2, "V"),
     ("ST", 1, 2, 2),
+    ("EO", 1, 3, 2, "V"),
+    ("ST", 1, 1, 2),
     ("ST", 1, 3, 2),
 ]
 

@@ -171,7 +171,6 @@ def tile_gatedgraphconvolution_pa_kernel(tc, adjacent, annotations, gc_bias, gru
         ps_tp = ctx.enter_context(tc.psum_pool(name="ps_tp", bufs=2))
         ps_s1 = ctx.enter_context(tc.psum_pool(name="ps_s1", bufs=2))
         ps_s2 = ctx.enter_context(tc.psum_pool(name="ps_s2", bufs=4))
-        ctx.enter_context(tc.manual_schedule())
 
         bv = keep.tile([P, 12], BF16, name="bv")
         gcb = keep.tile([P, 4], BF16, name="gcb")

@@ -9,344 +9,255 @@ U32 = mybir.dt.uint32
 U8 = mybir.dt.uint8
 FP8X4 = mybir.dt.float8_e4m3fn_x4
 ADD = mybir.AluOpType.add
-MULT = mybir.AluOpType.mult
-IDENT = mybir.ActivationFunctionType.Identity
+IDENTITY = mybir.ActivationFunctionType.Identity
 
 P = 128
-B, N, C, G = 2, 512, 512, 1536
-GT = G // 512
-FLOPS = 2 * B * N * N * C + 2 * B * N * C * G
+PACK = 4
+GRAPHS, NODES, CHANNELS, GATES = 2, 512, 512, 1536
+NODE_TILES = NODES // P
+CHANNEL_TILES = CHANNELS // P
+BANK = 512
+GATE_TILES = GATES // BANK
+HALF = 256
+BIAS_COLS = GATES // P
 
-ORDER = [
-    ("L_adj", 0),
-    ("d_gcb",),
-    ("d_brow",),
-    ("L_ann", 0),
-    ("L_W", 0),
-    ("ident",),
-    ("L_adj", 1),
-    ("L_ann", 1),
-    ("L_W", 1),
-    ("L_W", 2),
-    ("identb",),
-    ("gcf",),
-    ("T", 0, 0),
-    ("BX", 0),
-    ("EA", 0, 0, "S"),
-    ("T", 0, 1),
-    ("RA", 0, 1, "V"),
-    ("bx", 0, "S"),
-    ("BX", 1),
-    ("RA", 0, 0, "V"),
-    ("EA", 0, 1, "S"),
-    ("BX", 2),
-    ("RW", 0, 256, 256, "S"),
-    ("QA", 0, 0),
-    ("QA", 0, 1),
-    ("RW", 0, 0, 256, "V"),
-    ("T", 1, 1),
-    ("bx", 1, "S"),
-    ("QN", 0, 0),
-    ("QN", 0, 1),
-    ("T", 1, 0),
-    ("bx", 2, "S"),
-    ("QW", 0),
-    ("S1", 0, 0),
-    ("EA", 1, 1, "S"),
-    ("S1", 0, 1),
-    ("EM", 0, 0),
-    ("EA", 1, 0, "S"),
-    ("EM", 0, 1),
-    ("RA", 1, 0, "S"),
-    ("S1", 0, 2),
-    ("QM", 0, 0),
-    ("S1", 0, 3),
-    ("EM", 0, 2),
-    ("S2", 0, 0, 0),
-    ("RW", 1, 0, 256, "S"),
-    ("QM", 0, 1),
-    ("QM", 0, 2),
-    ("EO", 0, 0, 0, "V"),
-    ("S2", 0, 1, 0),
-    ("S2", 0, 2, 0),
-    ("QA", 1, 0),
-    ("RW", 1, 256, 256, "S"),
-    ("ST", 0, 0, 0),
-    ("QN", 1, 0),
-    ("QA", 1, 1),
-    ("EO", 0, 1, 0, "V"),
-    ("S1t", 1, 0),
-    ("RA", 1, 1, "S"),
-    ("QW", 1),
-    ("ST", 0, 1, 0),
-    ("EO", 0, 2, 0, "V"),
-    ("EMs", 1, 0),
-    ("S2", 0, 0, 1),
-    ("QN", 1, 1),
-    ("S2", 0, 1, 1),
-    ("ST", 0, 2, 0),
-    ("S2", 0, 2, 1),
-    ("EO", 0, 0, 1, "V"),
-    ("RW", 2, 0, 256, "S"),
-    ("EM", 0, 3),
-    ("ST", 0, 0, 1),
-    ("EO", 0, 2, 1, "V"),
-    ("RW", 2, 256, 256, "S"),
-    ("S1t", 1, 1),
-    ("S1t", 1, 2),
-    ("QM", 0, 3),
-    ("ST", 0, 2, 1),
-    ("EO", 0, 1, 1, "V"),
-    ("S2", 0, 3, 0),
-    ("EMs", 1, 1),
-    ("QW", 2),
-    ("S2", 0, 3, 1),
-    ("ST", 0, 1, 1),
-    ("EMs", 1, 2),
-    ("EO", 0, 3, 0, "V"),
-    ("S1t", 1, 3),
-    ("S2", 0, 0, 2),
-    ("EO", 0, 3, 1, "V"),
-    ("EMs", 1, 3),
-    ("S2", 0, 1, 2),
-    ("ST", 0, 3, 0),
-    ("S2", 0, 2, 2),
-    ("EO", 0, 0, 2, "V"),
-    ("ST", 0, 3, 1),
-    ("S2", 0, 3, 2),
-    ("RM", 1, 0, "S"),
-    ("EO", 0, 1, 2, "V"),
-    ("ST", 0, 0, 2),
-    ("EO", 0, 2, 2, "V"),
-    ("ST", 0, 1, 2),
-    ("RM", 1, 1, "S"),
-    ("QMh", 1, 0),
-    ("ST", 0, 2, 2),
-    ("EO", 0, 3, 2, "V"),
-    ("S2", 1, 0, 1),
-    ("S2", 1, 0, 0),
-    ("QMh", 1, 1),
-    ("ST", 0, 3, 2),
-    ("S2", 1, 1, 0),
-    ("EO", 1, 0, 1, "V"),
-    ("S2", 1, 1, 1),
-    ("EO", 1, 0, 0, "V"),
-    ("ST", 1, 0, 1),
-    ("S2", 1, 2, 0),
-    ("EO", 1, 1, 0, "V"),
-    ("S2", 1, 2, 1),
-    ("ST", 1, 0, 0),
-    ("EO", 1, 2, 0, "V"),
-    ("ST", 1, 1, 0),
-    ("S2", 1, 3, 0),
-    ("EO", 1, 1, 1, "V"),
-    ("ST", 1, 2, 0),
-    ("EO", 1, 3, 0, "V"),
-    ("S2", 1, 3, 1),
-    ("ST", 1, 1, 1),
-    ("S2", 1, 0, 2),
-    ("EO", 1, 2, 1, "V"),
-    ("ST", 1, 3, 0),
-    ("EO", 1, 3, 1, "V"),
-    ("ST", 1, 2, 1),
-    ("S2", 1, 1, 2),
-    ("S2", 1, 2, 2),
-    ("EO", 1, 0, 2, "V"),
-    ("ST", 1, 3, 1),
-    ("S2", 1, 3, 2),
-    ("EO", 1, 2, 2, "V"),
-    ("ST", 1, 0, 2),
-    ("EO", 1, 1, 2, "V"),
-    ("ST", 1, 2, 2),
-    ("EO", 1, 3, 2, "V"),
-    ("ST", 1, 1, 2),
-    ("ST", 1, 3, 2),
-]
+FLOPS = 2 * GRAPHS * NODES * NODES * CHANNELS + 2 * GRAPHS * NODES * CHANNELS * GATES
 
 
 def tile_gatedgraphconvolution_pa_kernel(tc, adjacent, annotations, gc_bias, gru_W, gru_b_x, out):
     nc = tc.nc
     with ExitStack() as ctx:
-        keep = ctx.enter_context(tc.tile_pool(name="keep", bufs=1))
-        ps_tp = ctx.enter_context(tc.psum_pool(name="ps_tp", bufs=2))
-        ps_s1 = ctx.enter_context(tc.psum_pool(name="ps_s1", bufs=2))
-        ps_s2 = ctx.enter_context(tc.psum_pool(name="ps_s2", bufs=4))
+        sbuf = ctx.enter_context(tc.tile_pool(name="sbuf", bufs=1))
+        psum_transposes = ctx.enter_context(tc.psum_pool(name="psum_transposes", bufs=2))
+        psum_stage1 = ctx.enter_context(tc.psum_pool(name="psum_stage1", bufs=2))
+        psum_stage2 = ctx.enter_context(tc.psum_pool(name="psum_stage2", bufs=4))
+        ctx.enter_context(tc.manual_schedule())
 
-        bv = keep.tile([P, 12], BF16, name="bv")
-        gcb = keep.tile([P, 4], BF16, name="gcb")
-        gcf = keep.tile([P, 4], F32, name="gcf")
-        ident = keep.tile([P, P], F32, name="ident")
-        identb = keep.tile([P, P], BF16, name="identb")
-        bx = keep.tile([P, G], F32, name="bx")
-        adj_raw = [keep.tile([P, 4 * N], BF16, name="adj_raw%d" % b) for b in range(B)]
-        ann_raw = [keep.tile([P, 4 * C], BF16, name="ann_raw%d" % b) for b in range(B)]
-        w_raw = [keep.tile([P, 4 * 512], BF16, name="w_raw%d" % g) for g in range(GT)]
-        msg_pl = [keep.tile([P, 4 * N], BF16, name="msg_pl%d" % b) for b in range(B)]
-        adj_grp = [keep.tile([P, 4 * N], BF16, name="adj_grp%d" % b, align_bytes=64) for b in range(B)]
-        ann_grp = [keep.tile([P, 4 * C], BF16, name="ann_grp%d" % b, align_bytes=64) for b in range(B)]
-        msg_grp = [keep.tile([P, 4 * N], BF16, name="msg_grp%d" % b, align_bytes=64) for b in range(B)]
-        w_grp = [keep.tile([P, 4 * 512], BF16, name="w_grp%d" % g, align_bytes=64) for g in range(GT)]
-        adj_q = [keep.tile([P, N], U32, name="adj_q%d" % b, align_bytes=64) for b in range(B)]
-        ann_q = [keep.tile([P, C], U32, name="ann_q%d" % b, align_bytes=64) for b in range(B)]
-        msg_q = [keep.tile([P, N], U32, name="msg_q%d" % b, align_bytes=64) for b in range(B)]
-        w_q = [keep.tile([P, 512], U32, name="w_q%d" % g, align_bytes=64) for g in range(GT)]
-        adj_s = [keep.tile([P, N], U8, name="adj_s%d" % b, align_bytes=64) for b in range(B)]
-        ann_s = [keep.tile([P, C], U8, name="ann_s%d" % b, align_bytes=64) for b in range(B)]
-        msg_s = [keep.tile([P, N], U8, name="msg_s%d" % b, align_bytes=64) for b in range(B)]
-        w_s = [keep.tile([P, 512], U8, name="w_s%d" % g, align_bytes=64) for g in range(GT)]
-        o_sb = keep.tile([P, B * 4 * G], F32, name="o_sb")
-        out_v = out.rearrange("(b p r) g -> b r p g", b=B, r=4)
-        live = {}
+        def operand(name, columns):
+            grouped = sbuf.tile([P, PACK * columns], BF16, name=name + "_grouped", align_bytes=64)
+            words = sbuf.tile([P, columns], U32, name=name + "_words", align_bytes=64)
+            scales = sbuf.tile([P, columns], U8, name=name + "_scales", align_bytes=64)
+            return grouped, words, scales
 
-        def copy_on(eng, dst, src):
-            if eng == "V":
-                nc.vector.tensor_copy(out=dst, in_=src)
-            elif eng == "S":
-                nc.scalar.copy(out=dst, in_=src)
-            else:
-                nc.gpsimd.tensor_scalar(out=dst, in0=src, scalar1=1.0, scalar2=0.0, op0=MULT, op1=ADD)
+        adj_rows = [sbuf.tile([P, NODE_TILES * NODES], BF16, name="adj_rows%d" % b) for b in range(GRAPHS)]
+        ann_planes = [sbuf.tile([P, PACK * CHANNELS], BF16, name="ann_planes%d" % b) for b in range(GRAPHS)]
+        w_planes = [sbuf.tile([P, PACK * BANK], BF16, name="w_planes%d" % g) for g in range(GATE_TILES)]
+        msg_planes = sbuf.tile([P, PACK * NODES], BF16, name="msg_planes")
+        adj = [operand("adj%d" % b, NODES) for b in range(GRAPHS)]
+        ann = [operand("ann%d" % b, CHANNELS) for b in range(GRAPHS)]
+        msg = [operand("msg%d" % b, NODES) for b in range(GRAPHS)]
+        w = [operand("w%d" % g, BANK) for g in range(GATE_TILES)]
+        identity_f32 = sbuf.tile([P, P], F32, name="identity_f32")
+        identity_bf16 = sbuf.tile([P, P], BF16, name="identity_bf16")
+        gc_bf16 = sbuf.tile([P, CHANNEL_TILES], BF16, name="gc_bf16")
+        gc_f32 = sbuf.tile([P, CHANNEL_TILES], F32, name="gc_f32")
+        gate_bias_cols = sbuf.tile([P, BIAS_COLS], BF16, name="gate_bias_cols")
+        gate_bias = sbuf.tile([P, GATES], F32, name="gate_bias")
+        result = sbuf.tile([P, GRAPHS * NODE_TILES * GATES], F32, name="result")
+        out_tiles = out.rearrange("(b p r) g -> b r p g", b=GRAPHS, r=NODE_TILES)
+        in_psum = {}
 
-        def quantise(grp, q, s, col0, ncol):
+        def quantise(mx_operand, first, count):
+            grouped, words, scales = mx_operand
             nc.vector.quantize_mx(
-                out=q[:, col0 : col0 + ncol].bitcast(FP8X4),
-                scales=s[:, col0 : col0 + ncol],
-                in_=grp[:, 4 * col0 : 4 * (col0 + ncol)],
+                out=words[:, first : first + count].bitcast(FP8X4),
+                scales=scales[:, first : first + count],
+                in_=grouped[:, PACK * first : PACK * (first + count)],
             )
 
-        def regroup(eng, grp, raw, col0, ncol):
-            dst = grp[:].rearrange("p (c i t) -> p c t i", i=4, t=4)
-            src = raw[:].rearrange("p (t c i) -> p c t i", t=4, i=4)
-            copy_on(eng, dst[:, col0 // 4 : (col0 + ncol) // 4], src[:, col0 // 4 : (col0 + ncol) // 4])
+        def regroup(copy, mx_operand, planes, first, count):
+            dst = mx_operand[0][:].rearrange("p (c i t) -> p c t i", i=4, t=PACK)
+            src = planes[:].rearrange("p (t c i) -> p c t i", t=PACK, i=4)
+            copy(out=dst[:, first // 4 : (first + count) // 4], in_=src[:, first // 4 : (first + count) // 4])
 
-        def mx(dst, lq, ls, lcols, rq, rs, rcols):
+        def mx_pass(acc, stationary, stationary_first, moving, moving_first, moving_count):
+            rows = slice(stationary_first, stationary_first + P)
+            cols = slice(moving_first, moving_first + moving_count)
             nc.tensor.matmul_mx(
-                out=dst,
-                lhsT=lq[:, lcols].bitcast(FP8X4),
-                lhsT_scale=ls[:, lcols],
-                rhs=rq[:, rcols].bitcast(FP8X4),
-                rhs_scale=rs[:, rcols],
+                out=acc,
+                lhsT=stationary[1][:, rows].bitcast(FP8X4),
+                lhsT_scale=stationary[2][:, rows],
+                rhs=moving[1][:, cols].bitcast(FP8X4),
+                rhs_scale=moving[2][:, cols],
                 start=True,
                 stop=True,
             )
 
-        def obank(b, r, g):
-            o0 = ((b * 4 + r) * GT + g) * 512
-            return o_sb[:, o0 : o0 + 512]
+        def load_adjacent(b, first_tile, tiles):
+            cols = slice(first_tile * NODES, (first_tile + tiles) * NODES)
+            nc.sync.dma_start(out=adj_rows[b][:, cols], in_=adjacent[b].rearrange("(p r) m -> p (r m)", r=NODE_TILES)[:, cols])
 
-        for op in ORDER:
-            k = op[0]
-            if k == "d_gcb":
-                with nc.allow_non_contiguous_dma(reason="512 bias values, one channel a partition"):
-                    nc.scalar.dma_start(out=gcb[:], in_=gc_bias.rearrange("a b (t p) -> p (a b t)", p=P))
-            elif k == "d_brow":
-                nc.scalar.dma_start(out=bv[:], in_=gru_b_x.rearrange("(p x) -> p x", x=12))
-            elif k == "ident":
-                masks.make_identity(nc, ident[:])
-            elif k == "identb":
-                nc.vector.tensor_copy(out=identb[:], in_=ident[:])
-            elif k == "gcf":
-                nc.vector.tensor_copy(out=gcf[:], in_=gcb[:])
-            elif k == "L_adj":
-                b = op[1]
-                nc.sync.dma_start(out=adj_raw[b][:], in_=adjacent[b].rearrange("(p r) m -> p (r m)", r=4))
-            elif k == "L_ann":
-                b = op[1]
-                nc.sync.dma_start(
-                    out=ann_raw[b][:].rearrange("q (u x) -> q u x", u=2),
-                    in_=annotations[b].rearrange("(u q e) c -> q u (e c)", u=2, e=2),
+        def load_annotations(b):
+            nc.sync.dma_start(
+                out=ann_planes[b][:].rearrange("q (u x) -> q u x", u=2),
+                in_=annotations[b].rearrange("(u q e) c -> q u (e c)", u=2, e=2),
+            )
+
+        def load_weights(g):
+            nc.sync.dma_start(
+                out=w_planes[g][:].rearrange("p (t x) -> p t x", t=PACK),
+                in_=gru_W[:, BANK * g : BANK * (g + 1)].rearrange("(t p) x -> p t x", p=P),
+            )
+
+        def spread_gate_bias(block):
+            spread = psum_stage2.tile([P, 4, P], F32, name="acc")
+            for i in range(4):
+                x = 4 * block + i
+                nc.tensor.matmul(
+                    out=spread[:, i, :],
+                    lhsT=gate_bias_cols[:, x : x + 1].to_broadcast([P, P]),
+                    rhs=identity_bf16[:],
+                    start=True,
+                    stop=True,
                 )
-            elif k == "L_W":
-                g = op[1]
-                nc.sync.dma_start(
-                    out=w_raw[g][:].rearrange("p (t x) -> p t x", t=4),
-                    in_=gru_W[:, 512 * g : 512 * g + 512].rearrange("(t p) x -> p t x", p=P),
-                )
-            elif k == "BX":
-                xb = op[1]
-                pb = ps_s2.tile([P, 4, P], F32, name="acc")
-                live[("BX", xb)] = pb
-                for xi in range(4):
-                    x = 4 * xb + xi
-                    nc.tensor.matmul(out=pb[:, xi, :], lhsT=bv[:, x : x + 1].to_broadcast([P, P]), rhs=identb[:], start=True, stop=True)
-            elif k == "bx":
-                xb, eng = op[1], op[2]
-                dst = bx[:].rearrange("m (n x) -> m n x", x=12)[:, :, 4 * xb : 4 * xb + 4]
-                copy_on(eng, dst, live[("BX", xb)][:].rearrange("m x n -> m n x"))
-            elif k == "T":
-                b, h = op[1], op[2]
-                words = adj_raw[b][:].bitcast(F32)
-                xt = ps_tp.tile([P, 2, 2, P], F32, name="xt")
-                live[("T", b, h)] = xt
-                for r2 in range(2):
-                    for u in range(2):
-                        w0 = (2 * h + r2) * 256 + u * 128
-                        nc.tensor.transpose(xt[:, r2, u, :], words[:, w0 : w0 + 128], ident[:])
-            elif k == "EA":
-                b, h, eng = op[1], op[2], op[3]
-                dst = adj_grp[b][:].bitcast(F32).rearrange("q (r p u) -> q r p u", r=4, u=2)
-                copy_on(eng, dst[:, 2 * h : 2 * h + 2], live[("T", b, h)][:].rearrange("q r u p -> q r p u"))
-            elif k == "QA":
-                b, h = op[1], op[2]
-                quantise(adj_grp[b], adj_q[b], adj_s[b], 256 * h, 256)
-            elif k == "RA":
-                b, h, eng = op[1], op[2], op[3]
-                regroup(eng, ann_grp[b], ann_raw[b], 256 * h, 256)
-            elif k == "QN":
-                b, h = op[1], op[2]
-                quantise(ann_grp[b], ann_q[b], ann_s[b], 256 * h, 256)
-            elif k == "RW":
-                g, c0, nco, eng = op[1], op[2], op[3], op[4]
-                regroup(eng, w_grp[g], w_raw[g], c0, nco)
-            elif k == "QW":
-                g = op[1]
-                quantise(w_grp[g], w_q[g], w_s[g], 0, 512)
-            elif k == "S1":
-                b, r = op[1], op[2]
-                bank = ps_s1.tile([P, 4, P], F32, name="bank")
-                live[("S1", b, r)] = bank
-                for t in range(4):
-                    mx(bank[:, t, :], ann_q[b], ann_s[b], slice(P * t, P * t + P), adj_q[b], adj_s[b], slice(P * r, P * r + P))
-            elif k == "EM":
-                b, r = op[1], op[2]
-                nc.vector.tensor_tensor(
-                    out=msg_grp[b][:, 4 * P * r : 4 * P * (r + 1)].rearrange("p (j t) -> p j t", t=4),
-                    in0=live[("S1", b, r)][:].rearrange("p t j -> p j t"),
-                    in1=gcb[:].unsqueeze(1).to_broadcast([P, P, 4]),
-                    op=ADD,
-                )
-            elif k == "QM":
-                b, r = op[1], op[2]
-                quantise(msg_grp[b], msg_q[b], msg_s[b], P * r, P)
-            elif k == "S1t":
-                b, t = op[1], op[2]
-                bank = ps_s1.tile([P, 512], F32, name="bank")
-                live[("S1t", b, t)] = bank
-                mx(bank[:], ann_q[b], ann_s[b], slice(P * t, P * t + P), adj_q[b], adj_s[b], slice(0, 512))
-            elif k == "EMs":
-                b, t = op[1], op[2]
-                nc.scalar.activation(out=msg_pl[b][:, 512 * t : 512 * t + 512], in_=live[("S1t", b, t)][:], func=IDENT, bias=gcf[:, t : t + 1], scale=1.0)
-            elif k == "RM":
-                b, h, eng = op[1], op[2], op[3]
-                regroup(eng, msg_grp[b], msg_pl[b], 256 * h, 256)
-            elif k == "QMh":
-                b, h = op[1], op[2]
-                quantise(msg_grp[b], msg_q[b], msg_s[b], 256 * h, 256)
-            elif k == "S2":
-                b, r, g = op[1], op[2], op[3]
-                acc = ps_s2.tile([P, 512], F32, name="acc")
-                live[("S2", b, r, g)] = acc
-                mx(acc[:], msg_q[b], msg_s[b], slice(P * r, P * r + P), w_q[g], w_s[g], slice(0, 512))
-            elif k == "EO":
-                b, r, g, eng = op[1], op[2], op[3], op[4]
-                if eng == "V":
-                    nc.vector.tensor_tensor(out=obank(b, r, g), in0=live[("S2", b, r, g)][:], in1=bx[:, 512 * g : 512 * g + 512], op=ADD)
-                else:
-                    nc.scalar.copy(out=obank(b, r, g), in_=live[("S2", b, r, g)][:])
-            elif k == "GA":
-                b, r, g = op[1], op[2], op[3]
-                nc.gpsimd.tensor_tensor(out=obank(b, r, g), in0=obank(b, r, g), in1=bx[:, 512 * g : 512 * g + 512], op=ADD)
-            elif k == "ST":
-                b, r, g = op[1], op[2], op[3]
-                nc.sync.dma_start(out=out_v[b, r, :, 512 * g : 512 * g + 512], in_=obank(b, r, g))
-            else:
-                assert False, k
+            nc.scalar.copy(
+                out=gate_bias[:].rearrange("m (n x) -> m n x", x=BIAS_COLS)[:, :, 4 * block : 4 * block + 4],
+                in_=spread[:].rearrange("m x n -> m n x"),
+            )
+
+        def transpose_adjacent(b, half):
+            pairs = adj_rows[b][:].bitcast(F32)
+            flipped = psum_transposes.tile([P, 2, 2, P], F32, name="flipped")
+            in_psum["flipped", b, half] = flipped
+            for r in range(2):
+                for u in range(2):
+                    first = (2 * half + r) * (NODES // 2) + u * P
+                    nc.tensor.transpose(flipped[:, r, u, :], pairs[:, first : first + P], identity_f32[:])
+
+        def collect_adjacent(b, half):
+            dst = adj[b][0][:].bitcast(F32).rearrange("q (r p u) -> q r p u", r=NODE_TILES, u=2)
+            nc.scalar.copy(
+                out=dst[:, 2 * half : 2 * half + 2],
+                in_=in_psum["flipped", b, half][:].rearrange("q r u p -> q r p u"),
+            )
+
+        def stage1_by_nodes(b, r):
+            bank = psum_stage1.tile([P, CHANNEL_TILES, P], F32, name="bank")
+            in_psum["by_nodes", b, r] = bank
+            for t in range(CHANNEL_TILES):
+                mx_pass(bank[:, t, :], ann[b], P * t, adj[b], P * r, P)
+
+        def msg_by_nodes(b, r):
+            nc.vector.tensor_tensor(
+                out=msg[b][0][:, PACK * P * r : PACK * P * (r + 1)].rearrange("p (j t) -> p j t", t=PACK),
+                in0=in_psum["by_nodes", b, r][:].rearrange("p t j -> p j t"),
+                in1=gc_f32[:].unsqueeze(1).to_broadcast([P, P, PACK]),
+                op=ADD,
+            )
+
+        def stage1_by_channels(b, t):
+            bank = psum_stage1.tile([P, NODES], F32, name="bank")
+            in_psum["by_channels", b, t] = bank
+            mx_pass(bank[:], ann[b], P * t, adj[b], 0, NODES)
+
+        def msg_by_channels(b, t):
+            nc.scalar.activation(
+                out=msg_planes[:, NODES * t : NODES * (t + 1)],
+                in_=in_psum["by_channels", b, t][:],
+                func=IDENTITY,
+                bias=gc_f32[:, t : t + 1],
+                scale=1.0,
+            )
+
+        banks = [(b, g, r) for b in range(GRAPHS) for g in range(GATE_TILES) for r in range(NODE_TILES)]
+
+        def stage2(b, g, r):
+            acc = psum_stage2.tile([P, BANK], F32, name="acc")
+            in_psum["acc", b, g, r] = acc
+            mx_pass(acc[:], msg[b], P * r, w[g], 0, BANK)
+
+        def finish(b, g, r):
+            first = (b * NODE_TILES + r) * GATES + g * BANK
+            nc.vector.tensor_tensor(
+                out=result[:, first : first + BANK],
+                in0=in_psum["acc", b, g, r][:],
+                in1=gate_bias[:, BANK * g : BANK * (g + 1)],
+                op=ADD,
+            )
+            nc.sync.dma_start(out=out_tiles[b, r, :, BANK * g : BANK * (g + 1)], in_=result[:, first : first + BANK])
+
+        with nc.allow_non_contiguous_dma(reason="512 values of gc_bias, channel 128 t + p to partition p"):
+            nc.scalar.dma_start(out=gc_bf16[:], in_=gc_bias.rearrange("a b (t p) -> p (a b t)", p=P))
+        nc.sync.dma_start(out=gate_bias_cols[:], in_=gru_b_x.rearrange("(p x) -> p x", x=BIAS_COLS))
+        load_annotations(0)
+        load_adjacent(0, 0, 2)
+        load_adjacent(0, 2, 2)
+        load_weights(0)
+        load_adjacent(1, 0, NODE_TILES)
+        load_annotations(1)
+        load_weights(1)
+        load_weights(2)
+
+        masks.make_identity(nc, identity_f32[:])
+        nc.vector.tensor_copy(out=identity_bf16[:], in_=identity_f32[:])
+        for block in range(BIAS_COLS // 4):
+            spread_gate_bias(block)
+
+        for half in range(2):
+            regroup(nc.vector.tensor_copy, ann[0], ann_planes[0], HALF * half, HALF)
+        for half in range(2):
+            quantise(ann[0], HALF * half, HALF)
+        nc.vector.tensor_copy(out=gc_f32[:], in_=gc_bf16[:])
+        for half in range(2):
+            transpose_adjacent(0, half)
+        for half in range(2):
+            collect_adjacent(0, half)
+        for half in range(2):
+            quantise(adj[0], HALF * half, HALF)
+        regroup(nc.vector.tensor_copy, w[0], w_planes[0], 0, HALF)
+        regroup(nc.scalar.copy, w[0], w_planes[0], HALF, HALF)
+
+        stage1_by_nodes(0, 0)
+        stage1_by_nodes(0, 1)
+        for half in range(2):
+            transpose_adjacent(1, half)
+        for half in range(2):
+            collect_adjacent(1, half)
+        regroup(nc.scalar.copy, ann[1], ann_planes[1], 0, HALF)
+        for half in range(2):
+            regroup(nc.scalar.copy, w[1], w_planes[1], HALF * half, HALF)
+        regroup(nc.scalar.copy, ann[1], ann_planes[1], HALF, HALF)
+        msg_by_nodes(0, 0)
+        stage1_by_nodes(0, 2)
+        msg_by_nodes(0, 1)
+        stage1_by_nodes(0, 3)
+        quantise(w[0], 0, BANK)
+        quantise(msg[0], 0, P)
+        msg_by_nodes(0, 2)
+        quantise(msg[0], P, P)
+        msg_by_nodes(0, 3)
+        quantise(msg[0], 2 * P, P)
+        quantise(msg[0], 3 * P, P)
+
+        woven = {
+            0: [(quantise, adj[1], 0, HALF), (quantise, adj[1], HALF, HALF), (quantise, ann[1], 0, HALF)],
+            1: [(quantise, w[1], 0, BANK)],
+            2: [
+                (quantise, ann[1], HALF, HALF),
+                (stage1_by_channels, 1, 0),
+                (stage1_by_channels, 1, 1),
+                (msg_by_channels, 1, 0),
+                (regroup, nc.scalar.copy, w[2], w_planes[2], 0, HALF),
+                (regroup, nc.scalar.copy, w[2], w_planes[2], HALF, HALF),
+                (msg_by_channels, 1, 1),
+            ],
+            5: [(stage1_by_channels, 1, 2), (msg_by_channels, 1, 2)],
+            6: [
+                (quantise, w[2], 0, BANK),
+                (stage1_by_channels, 1, 3),
+                (msg_by_channels, 1, 3),
+                (regroup, nc.scalar.copy, msg[1], msg_planes, 0, HALF),
+                (regroup, nc.scalar.copy, msg[1], msg_planes, HALF, HALF),
+            ],
+            10: [(quantise, msg[1], 0, HALF)],
+            11: [(quantise, msg[1], HALF, HALF)],
+        }
+        ahead = 2
+        for bank in banks[:ahead]:
+            stage2(*bank)
+        for i, bank in enumerate(banks):
+            finish(*bank)
+            for step in woven.get(i, []):
+                step[0](*step[1:])
+            if i + ahead < len(banks):
+                stage2(*banks[i + ahead])

@@ -176,9 +176,9 @@ def tile_gatedgraphconvolution_pa_kernel(tc, adjacent, annotations, gc_bias, gru
             )
             nc.sync.dma_start(out=out_tiles[b, r, :, BANK * g : BANK * (g + 1)], in_=result[:, first : first + BANK])
 
-        with nc.allow_non_contiguous_dma(reason="512 values of gc_bias, channel 128 t + p to partition p"):
-            nc.scalar.dma_start(out=gc_bf16[:], in_=gc_bias.rearrange("a b (t p) -> p (a b t)", p=P))
         nc.sync.dma_start(out=gate_bias_cols[:], in_=gru_b_x.rearrange("(p x) -> p x", x=BIAS_COLS))
+        with nc.allow_non_contiguous_dma(reason="512 values of gc_bias, channel 128 t + p to partition p"):
+            nc.sync.dma_start(out=gc_bf16[:], in_=gc_bias.rearrange("a b (t p) -> p (a b t)", p=P))
         load_annotations(0)
         load_adjacent(0, 0, 2)
         load_adjacent(0, 2, 2)
@@ -197,7 +197,6 @@ def tile_gatedgraphconvolution_pa_kernel(tc, adjacent, annotations, gc_bias, gru
             regroup(nc.vector.tensor_copy, ann[0], ann_planes[0], HALF * half, HALF)
         for half in range(2):
             quantise(ann[0], HALF * half, HALF)
-        nc.vector.tensor_copy(out=gc_f32[:], in_=gc_bf16[:])
         for half in range(2):
             transpose_adjacent(0, half)
         for half in range(2):
@@ -206,6 +205,7 @@ def tile_gatedgraphconvolution_pa_kernel(tc, adjacent, annotations, gc_bias, gru
             quantise(adj[0], HALF * half, HALF)
         regroup(nc.vector.tensor_copy, w[0], w_planes[0], 0, HALF)
         regroup(nc.scalar.copy, w[0], w_planes[0], HALF, HALF)
+        nc.vector.tensor_copy(out=gc_f32[:], in_=gc_bf16[:])
 
         stage1_by_nodes(0, 0)
         stage1_by_nodes(0, 1)

@@ -9,6 +9,7 @@ U32 = mybir.dt.uint32
 U8 = mybir.dt.uint8
 FP8X4 = mybir.dt.float8_e4m3fn_x4
 ADD = mybir.AluOpType.add
+MULT = mybir.AluOpType.mult
 IDENTITY = mybir.ActivationFunctionType.Identity
 
 P = 128
@@ -20,6 +21,7 @@ BANK = 512
 GATE_TILES = GATES // BANK
 HALF = 256
 BIAS_COLS = GATES // P
+AHEAD = 2
 
 FLOPS = 2 * GRAPHS * NODES * NODES * CHANNELS + 2 * GRAPHS * NODES * CHANNELS * GATES
 
@@ -69,6 +71,9 @@ def tile_gatedgraphconvolution_pa_kernel(tc, adjacent, annotations, gc_bias, gru
             dst = mx_operand[0][:].rearrange("p (c i t) -> p c t i", i=4, t=PACK)
             src = planes[:].rearrange("p (t c i) -> p c t i", t=PACK, i=4)
             copy(out=dst[:, first // 4 : (first + count) // 4], in_=src[:, first // 4 : (first + count) // 4])
+
+        def gpsimd_copy(out, in_):
+            nc.gpsimd.tensor_scalar(out=out, in0=in_, scalar1=1.0, scalar2=0.0, op0=MULT, op1=ADD)
 
         def mx_pass(acc, stationary, stationary_first, moving, moving_first, moving_count):
             rows = slice(stationary_first, stationary_first + P)
@@ -217,6 +222,8 @@ def tile_gatedgraphconvolution_pa_kernel(tc, adjacent, annotations, gc_bias, gru
         for half in range(2):
             regroup(nc.scalar.copy, w[1], w_planes[1], HALF * half, HALF)
         regroup(nc.scalar.copy, ann[1], ann_planes[1], HALF, HALF)
+        for piece in range(BANK // P):
+            regroup(gpsimd_copy, w[2], w_planes[2], P * piece, P)
         msg_by_nodes(0, 0)
         stage1_by_nodes(0, 2)
         msg_by_nodes(0, 1)
@@ -229,35 +236,60 @@ def tile_gatedgraphconvolution_pa_kernel(tc, adjacent, annotations, gc_bias, gru
         quantise(msg[0], 2 * P, P)
         quantise(msg[0], 3 * P, P)
 
-        woven = {
-            0: [(quantise, adj[1], 0, HALF), (quantise, adj[1], HALF, HALF), (quantise, ann[1], 0, HALF)],
-            1: [(quantise, w[1], 0, BANK)],
-            2: [
-                (quantise, ann[1], HALF, HALF),
-                (stage1_by_channels, 1, 0),
-                (stage1_by_channels, 1, 1),
-                (msg_by_channels, 1, 0),
-                (regroup, nc.scalar.copy, w[2], w_planes[2], 0, HALF),
-                (regroup, nc.scalar.copy, w[2], w_planes[2], HALF, HALF),
-                (msg_by_channels, 1, 1),
-            ],
-            5: [(stage1_by_channels, 1, 2), (msg_by_channels, 1, 2)],
-            6: [
-                (quantise, w[2], 0, BANK),
-                (stage1_by_channels, 1, 3),
-                (msg_by_channels, 1, 3),
-                (regroup, nc.scalar.copy, msg[1], msg_planes, 0, HALF),
-                (regroup, nc.scalar.copy, msg[1], msg_planes, HALF, HALF),
-            ],
-            10: [(quantise, msg[1], 0, HALF)],
-            11: [(quantise, msg[1], HALF, HALF)],
-        }
-        ahead = 2
-        for bank in banks[:ahead]:
-            stage2(*bank)
-        for i, bank in enumerate(banks):
-            finish(*bank)
-            for step in woven.get(i, []):
-                step[0](*step[1:])
-            if i + ahead < len(banks):
-                stage2(*banks[i + ahead])
+        def start_bank(i):
+            if i < len(banks):
+                stage2(*banks[i])
+
+        def stream(first, stop):
+            for i in range(first, stop):
+                finish(*banks[i])
+                start_bank(i + AHEAD)
+
+        for i in range(AHEAD):
+            start_bank(i)
+
+        finish(*banks[0])
+        for half in range(2):
+            quantise(adj[1], HALF * half, HALF)
+        quantise(ann[1], 0, HALF)
+        start_bank(0 + AHEAD)
+
+        finish(*banks[1])
+        quantise(w[1], 0, BANK)
+        start_bank(1 + AHEAD)
+
+        finish(*banks[2])
+        quantise(ann[1], HALF, HALF)
+        stage1_by_channels(1, 0)
+        stage1_by_channels(1, 1)
+        msg_by_channels(1, 0)
+        msg_by_channels(1, 1)
+        start_bank(2 + AHEAD)
+
+        finish(*banks[3])
+        stage1_by_channels(1, 2)
+        msg_by_channels(1, 2)
+        start_bank(3 + AHEAD)
+
+        finish(*banks[4])
+        stage1_by_channels(1, 3)
+        msg_by_channels(1, 3)
+        for half in range(2):
+            regroup(nc.scalar.copy, msg[1], msg_planes, HALF * half, HALF)
+        start_bank(4 + AHEAD)
+
+        finish(*banks[5])
+        quantise(w[2], 0, BANK)
+        start_bank(5 + AHEAD)
+
+        stream(6, 8)
+
+        finish(*banks[8])
+        quantise(msg[1], 0, HALF)
+        start_bank(8 + AHEAD)
+
+        finish(*banks[9])
+        quantise(msg[1], HALF, HALF)
+        start_bank(9 + AHEAD)
+
+        stream(10, len(banks))

from contextlib import ExitStack

import concourse.masks as masks
import concourse.mybir as mybir

F32 = mybir.dt.float32
BF16 = mybir.dt.bfloat16
U32 = mybir.dt.uint32
U8 = mybir.dt.uint8
FP8X4 = mybir.dt.float8_e4m3fn_x4
ADD = mybir.AluOpType.add
MULT = mybir.AluOpType.mult
IDENTITY = mybir.ActivationFunctionType.Identity

P = 128
PACK = 4
GRAPHS, NODES, CHANNELS, GATES = 2, 512, 512, 1536
NODE_TILES = NODES // P
CHANNEL_TILES = CHANNELS // P
BANK = 512
GATE_TILES = GATES // BANK
HALF = 256
BIAS_COLS = GATES // P
AHEAD = 2

FLOPS = 2 * GRAPHS * NODES * NODES * CHANNELS + 2 * GRAPHS * NODES * CHANNELS * GATES


def tile_gatedgraphconvolution_pa_kernel(tc, adjacent, annotations, gc_bias, gru_W, gru_b_x, out):
    nc = tc.nc
    with ExitStack() as ctx:
        sbuf = ctx.enter_context(tc.tile_pool(name="sbuf", bufs=1))
        psum_transposes = ctx.enter_context(tc.psum_pool(name="psum_transposes", bufs=2))
        psum_stage1 = ctx.enter_context(tc.psum_pool(name="psum_stage1", bufs=2))
        psum_stage2 = ctx.enter_context(tc.psum_pool(name="psum_stage2", bufs=4))
        ctx.enter_context(tc.manual_schedule())

        def operand(name, columns):
            grouped = sbuf.tile([P, PACK * columns], BF16, name=name + "_grouped", align_bytes=64)
            words = sbuf.tile([P, columns], U32, name=name + "_words", align_bytes=64)
            scales = sbuf.tile([P, columns], U8, name=name + "_scales", align_bytes=64)
            return grouped, words, scales

        adj_rows = [sbuf.tile([P, NODE_TILES * NODES], BF16, name="adj_rows%d" % b) for b in range(GRAPHS)]
        ann_planes = [sbuf.tile([P, PACK * CHANNELS], BF16, name="ann_planes%d" % b) for b in range(GRAPHS)]
        w_planes = [sbuf.tile([P, PACK * BANK], BF16, name="w_planes%d" % g) for g in range(GATE_TILES)]
        msg_planes = sbuf.tile([P, PACK * NODES], BF16, name="msg_planes")
        adj = [operand("adj%d" % b, NODES) for b in range(GRAPHS)]
        ann = [operand("ann%d" % b, CHANNELS) for b in range(GRAPHS)]
        msg = [operand("msg%d" % b, NODES) for b in range(GRAPHS)]
        w = [operand("w%d" % g, BANK) for g in range(GATE_TILES)]
        identity_f32 = sbuf.tile([P, P], F32, name="identity_f32")
        identity_bf16 = sbuf.tile([P, P], BF16, name="identity_bf16")
        gc_bf16 = sbuf.tile([P, CHANNEL_TILES], BF16, name="gc_bf16")
        gc_f32 = sbuf.tile([P, CHANNEL_TILES], F32, name="gc_f32")
        gate_bias_cols = sbuf.tile([P, BIAS_COLS], BF16, name="gate_bias_cols")
        gate_bias = sbuf.tile([P, GATES], F32, name="gate_bias")
        result = sbuf.tile([P, GRAPHS * NODE_TILES * GATES], F32, name="result")
        out_tiles = out.rearrange("(b p r) g -> b r p g", b=GRAPHS, r=NODE_TILES)
        in_psum = {}

        def quantise(mx_operand, first, count):
            grouped, words, scales = mx_operand
            nc.vector.quantize_mx(
                out=words[:, first : first + count].bitcast(FP8X4),
                scales=scales[:, first : first + count],
                in_=grouped[:, PACK * first : PACK * (first + count)],
            )

        def regroup(copy, mx_operand, planes, first, count):
            dst = mx_operand[0][:].rearrange("p (c i t) -> p c t i", i=4, t=PACK)
            src = planes[:].rearrange("p (t c i) -> p c t i", t=PACK, i=4)
            copy(out=dst[:, first // 4 : (first + count) // 4], in_=src[:, first // 4 : (first + count) // 4])

        def gpsimd_copy(out, in_):
            nc.gpsimd.tensor_scalar(out=out, in0=in_, scalar1=1.0, scalar2=0.0, op0=MULT, op1=ADD)

        def mx_pass(acc, stationary, stationary_first, moving, moving_first, moving_count):
            rows = slice(stationary_first, stationary_first + P)
            cols = slice(moving_first, moving_first + moving_count)
            nc.tensor.matmul_mx(
                out=acc,
                lhsT=stationary[1][:, rows].bitcast(FP8X4),
                lhsT_scale=stationary[2][:, rows],
                rhs=moving[1][:, cols].bitcast(FP8X4),
                rhs_scale=moving[2][:, cols],
                start=True,
                stop=True,
            )

        def load_adjacent(b, first_tile, tiles):
            cols = slice(first_tile * NODES, (first_tile + tiles) * NODES)
            nc.sync.dma_start(out=adj_rows[b][:, cols], in_=adjacent[b].rearrange("(p r) m -> p (r m)", r=NODE_TILES)[:, cols])

        def load_annotations(b):
            nc.sync.dma_start(
                out=ann_planes[b][:].rearrange("q (u x) -> q u x", u=2),
                in_=annotations[b].rearrange("(u q e) c -> q u (e c)", u=2, e=2),
            )

        def load_weights(g):
            nc.sync.dma_start(
                out=w_planes[g][:].rearrange("p (t x) -> p t x", t=PACK),
                in_=gru_W[:, BANK * g : BANK * (g + 1)].rearrange("(t p) x -> p t x", p=P),
            )

        def spread_gate_bias(block):
            spread = psum_stage2.tile([P, 4, P], F32, name="acc")
            for i in range(4):
                x = 4 * block + i
                nc.tensor.matmul(
                    out=spread[:, i, :],
                    lhsT=gate_bias_cols[:, x : x + 1].to_broadcast([P, P]),
                    rhs=identity_bf16[:],
                    start=True,
                    stop=True,
                )
            nc.scalar.copy(
                out=gate_bias[:].rearrange("m (n x) -> m n x", x=BIAS_COLS)[:, :, 4 * block : 4 * block + 4],
                in_=spread[:].rearrange("m x n -> m n x"),
            )

        def transpose_adjacent(b, half):
            pairs = adj_rows[b][:].bitcast(F32)
            flipped = psum_transposes.tile([P, 2, 2, P], F32, name="flipped")
            in_psum["flipped", b, half] = flipped
            for r in range(2):
                for u in range(2):
                    first = (2 * half + r) * (NODES // 2) + u * P
                    nc.tensor.transpose(flipped[:, r, u, :], pairs[:, first : first + P], identity_f32[:])

        def collect_adjacent(b, half):
            dst = adj[b][0][:].bitcast(F32).rearrange("q (r p u) -> q r p u", r=NODE_TILES, u=2)
            nc.scalar.copy(
                out=dst[:, 2 * half : 2 * half + 2],
                in_=in_psum["flipped", b, half][:].rearrange("q r u p -> q r p u"),
            )

        def stage1_by_nodes(b, r):
            bank = psum_stage1.tile([P, CHANNEL_TILES, P], F32, name="bank")
            in_psum["by_nodes", b, r] = bank
            for t in range(CHANNEL_TILES):
                mx_pass(bank[:, t, :], ann[b], P * t, adj[b], P * r, P)

        def msg_by_nodes(b, r):
            nc.vector.tensor_tensor(
                out=msg[b][0][:, PACK * P * r : PACK * P * (r + 1)].rearrange("p (j t) -> p j t", t=PACK),
                in0=in_psum["by_nodes", b, r][:].rearrange("p t j -> p j t"),
                in1=gc_f32[:].unsqueeze(1).to_broadcast([P, P, PACK]),
                op=ADD,
            )

        def stage1_by_channels(b, t):
            bank = psum_stage1.tile([P, NODES], F32, name="bank")
            in_psum["by_channels", b, t] = bank
            mx_pass(bank[:], ann[b], P * t, adj[b], 0, NODES)

        def msg_by_channels(b, t):
            nc.scalar.activation(
                out=msg_planes[:, NODES * t : NODES * (t + 1)],
                in_=in_psum["by_channels", b, t][:],
                func=IDENTITY,
                bias=gc_f32[:, t : t + 1],
                scale=1.0,
            )

        banks = [(b, g, r) for b in range(GRAPHS) for g in range(GATE_TILES) for r in range(NODE_TILES)]

        def stage2(b, g, r):
            acc = psum_stage2.tile([P, BANK], F32, name="acc")
            in_psum["acc", b, g, r] = acc
            mx_pass(acc[:], msg[b], P * r, w[g], 0, BANK)

        def finish(b, g, r):
            first = (b * NODE_TILES + r) * GATES + g * BANK
            nc.vector.tensor_tensor(
                out=result[:, first : first + BANK],
                in0=in_psum["acc", b, g, r][:],
                in1=gate_bias[:, BANK * g : BANK * (g + 1)],
                op=ADD,
            )
            nc.sync.dma_start(out=out_tiles[b, r, :, BANK * g : BANK * (g + 1)], in_=result[:, first : first + BANK])

        nc.sync.dma_start(out=gate_bias_cols[:], in_=gru_b_x.rearrange("(p x) -> p x", x=BIAS_COLS))
        with nc.allow_non_contiguous_dma(reason="512 values of gc_bias, channel 128 t + p to partition p"):
            nc.sync.dma_start(out=gc_bf16[:], in_=gc_bias.rearrange("a b (t p) -> p (a b t)", p=P))
        load_annotations(0)
        load_adjacent(0, 0, 2)
        load_adjacent(0, 2, 2)
        load_weights(0)
        load_adjacent(1, 0, NODE_TILES)
        load_annotations(1)
        load_weights(1)
        load_weights(2)

        masks.make_identity(nc, identity_f32[:])
        nc.vector.tensor_copy(out=identity_bf16[:], in_=identity_f32[:])
        for block in range(BIAS_COLS // 4):
            spread_gate_bias(block)

        for half in range(2):
            regroup(nc.vector.tensor_copy, ann[0], ann_planes[0], HALF * half, HALF)
        for half in range(2):
            quantise(ann[0], HALF * half, HALF)
        for half in range(2):
            transpose_adjacent(0, half)
        for half in range(2):
            collect_adjacent(0, half)
        for half in range(2):
            quantise(adj[0], HALF * half, HALF)
        regroup(nc.vector.tensor_copy, w[0], w_planes[0], 0, HALF)
        regroup(nc.scalar.copy, w[0], w_planes[0], HALF, HALF)
        nc.vector.tensor_copy(out=gc_f32[:], in_=gc_bf16[:])

        stage1_by_nodes(0, 0)
        stage1_by_nodes(0, 1)
        for half in range(2):
            transpose_adjacent(1, half)
        for half in range(2):
            collect_adjacent(1, half)
        regroup(nc.scalar.copy, ann[1], ann_planes[1], 0, HALF)
        for half in range(2):
            regroup(nc.scalar.copy, w[1], w_planes[1], HALF * half, HALF)
        regroup(nc.scalar.copy, ann[1], ann_planes[1], HALF, HALF)
        for piece in range(BANK // P):
            regroup(gpsimd_copy, w[2], w_planes[2], P * piece, P)
        msg_by_nodes(0, 0)
        stage1_by_nodes(0, 2)
        msg_by_nodes(0, 1)
        stage1_by_nodes(0, 3)
        quantise(w[0], 0, BANK)
        quantise(msg[0], 0, P)
        msg_by_nodes(0, 2)
        quantise(msg[0], P, P)
        msg_by_nodes(0, 3)
        quantise(msg[0], 2 * P, P)
        quantise(msg[0], 3 * P, P)

        def start_bank(i):
            if i < len(banks):
                stage2(*banks[i])

        def stream(first, stop):
            for i in range(first, stop):
                finish(*banks[i])
                start_bank(i + AHEAD)

        for i in range(AHEAD):
            start_bank(i)

        finish(*banks[0])
        for half in range(2):
            quantise(adj[1], HALF * half, HALF)
        quantise(ann[1], 0, HALF)
        start_bank(0 + AHEAD)

        finish(*banks[1])
        quantise(w[1], 0, BANK)
        start_bank(1 + AHEAD)

        finish(*banks[2])
        quantise(ann[1], HALF, HALF)
        stage1_by_channels(1, 0)
        stage1_by_channels(1, 1)
        msg_by_channels(1, 0)
        msg_by_channels(1, 1)
        start_bank(2 + AHEAD)

        finish(*banks[3])
        stage1_by_channels(1, 2)
        msg_by_channels(1, 2)
        start_bank(3 + AHEAD)

        finish(*banks[4])
        stage1_by_channels(1, 3)
        msg_by_channels(1, 3)
        for half in range(2):
            regroup(nc.scalar.copy, msg[1], msg_planes, HALF * half, HALF)
        start_bank(4 + AHEAD)

        finish(*banks[5])
        quantise(w[2], 0, BANK)
        start_bank(5 + AHEAD)

        stream(6, 8)

        finish(*banks[8])
        quantise(msg[1], 0, HALF)
        start_bank(8 + AHEAD)

        finish(*banks[9])
        quantise(msg[1], HALF, HALF)
        start_bank(9 + AHEAD)

        stream(10, len(banks))
